import numpy as np
import ml_dtypes


def mxq(x, axis, fmt="e4m3"):
    dtype, down = {"e4m3": (ml_dtypes.float8_e4m3fn, 7), "e5m2": (ml_dtypes.float8_e5m2, 14)}[fmt]
    v = np.moveaxis(np.asarray(x, np.float32).astype(ml_dtypes.bfloat16).astype(np.float64), axis, -1)
    blocks = v.reshape(v.shape[:-1] + (-1, 32))
    amax = np.abs(blocks).max(-1, keepdims=True)
    byte = np.maximum(np.where(amax > 0, np.frexp(amax)[1] - 1 + 127, 0) - down, 1)
    scale = np.exp2(byte - 127.0)
    codes = (blocks / scale).astype(np.float32).astype(dtype).astype(np.float64)
    return np.moveaxis((codes * scale).reshape(v.shape), -1, axis)


WIDE = False


def mx_kscale(k):
    if not WIDE:
        return np.ones(k)
    levels = np.array([20, -20, 10, -10, 0])
    a = np.random.permutation(np.resize(levels, k // 512 * 4)).reshape(k // 512, 4)
    idx = np.arange(k)
    return np.exp2(a[idx // 512, idx % 128 // 32])


BF16 = ml_dtypes.bfloat16


def bf(x):
    return np.asarray(x, np.float32).astype(BF16)


def f64(x):
    return np.asarray(x).astype(np.float64)


B, T, G, I, H = 2, 1024, 4, 512, 512


def setup_inputs():
    u = mx_kscale(H)
    x = np.random.standard_normal((B, T, G, I)).reshape(B, T, G * I)
    W = np.random.standard_normal((G, H, I)) / np.sqrt(I) / u[None, :, None]
    b = np.random.standard_normal((G, H)) * 0.5
    g = (np.random.standard_normal((B, T, H, G))
         * np.exp2(np.random.randint(-12, 1, (B, T, 1, 1))) * 4.0 * u[:, None])
    return {"x": bf(x), "W": bf(W), "b": bf(b), "grad_out": bf(g.reshape(B, T, H * G))}


def reference(x, W, b, grad_out):
    gy = f64(grad_out).reshape(B, T, H, G).transpose(3, 0, 1, 2).reshape(G, B * T, H)
    gq = mxq(gy, 2, "e5m2")
    wq = mxq(f64(W), 1, "e4m3")
    gx = gq @ wq
    return gx.reshape(G, B, T, I).transpose(1, 2, 0, 3).reshape(B, T, G * I)

@@ -1,0 +1,190 @@
+from contextlib import ExitStack
+
+import concourse.mybir as mybir
+from concourse.masks import make_identity
+
+F32 = mybir.dt.float32
+BF16 = mybir.dt.bfloat16
+U32 = mybir.dt.uint32
+U8 = mybir.dt.uint8
+E4M3X4 = mybir.dt.float8_e4m3fn_x4
+E5M2X4 = mybir.dt.float8_e5m2_x4
+
+P = 128
+PACK = 4
+G = 4
+H = 512
+I = 512
+TOKENS = 2048
+NT = TOKENS // P
+COLS = G * H
+
+FLOPS = 2 * TOKENS * G * H * I
+BYTES = TOKENS * COLS * 2 + G * H * I * 2 + TOKENS * G * I * 4
+
+LOADS = (
+    ("g", 0, 1), ("w", 0, 1), ("w", 1, 1), ("g", 1, 1), ("w", 2, 1), ("w", 3, 1),
+    ("g", 2, 1), ("g", 3, 1), ("g", 4, 2), ("g", 6, 2), ("g", 8, 4), ("g", 12, 4),
+)
+XT_BANKS = 4
+ACC_BANKS = 4
+GROUPED_BUFS = 4
+CODES_BUFS = 4
+STAGE_BUFS = 10
+AHEAD = 2
+
+
+def scalar_takes_out(j, g):
+    if j == 0:
+        return True
+    if j >= NT - 2:
+        return g >= 2
+    return g == 3 and j % 2 == 1
+
+
+def tile_groupedlinear_t_kernel(tc, x, W, b, grad_out, out):
+    nc = tc.nc
+    g_rows = grad_out.flatten_outer_dims().rearrange("(p j) c -> p j c", j=NT)
+    o_rows = out.flatten_outer_dims().rearrange("(p j) c -> p j c", j=NT)
+
+    with ExitStack() as ctx:
+        keep = ctx.enter_context(tc.tile_pool(name="keep", bufs=1))
+        ring = ctx.enter_context(tc.tile_pool(name="ring", bufs=1))
+        psum = ctx.enter_context(tc.psum_pool(name="psum", bufs=1))
+        ctx.enter_context(tc.manual_schedule())
+
+        g_words = {}
+        w_raw = {}
+        for kind, first, count in LOADS:
+            if kind == "g":
+                g_in = keep.tile([P, count * COLS], BF16, name="g_in%d" % first)
+                nc.sync.dma_start(
+                    out=g_in[:].rearrange("p (n c) -> p n c", n=count),
+                    in_=g_rows[:, first : first + count, :],
+                )
+                words = g_in[:].bitcast(F32).rearrange(
+                    "p (n t h q) -> p n t h q", n=count, t=PACK, h=P, q=2
+                )
+                for n in range(count):
+                    g_words[first + n] = words[:, n, :, :, :]
+            else:
+                raw = keep.tile([P, PACK * I], BF16, name="w_raw%d" % first)
+                nc.sync.dma_start(
+                    out=raw[:].rearrange("p (t i) -> p t i", t=PACK),
+                    in_=W[first, :, :].rearrange("(t p) i -> p t i", p=P),
+                )
+                w_raw[first] = raw
+
+        ident = keep.tile([P, P], F32, name="ident")
+        make_identity(nc, ident[:])
+        w_codes = keep.tile([P, G * I], U32, name="w_codes", align_bytes=64)
+        w_scales = keep.tile([P, G * I], U8, name="w_scales", align_bytes=64)
+
+        xt_of = {}
+        grouped_of = {}
+        codes_of = {}
+        acc_of = {}
+        stage_of = {}
+
+        def transposes(j, pair):
+            unit = 2 * j + pair
+            xt = psum.tile([P, PACK * P], F32, name="xt", tag="xt%d" % (unit % XT_BANKS))
+            for t in range(PACK):
+                nc.tensor.transpose(xt[:, t * P : (t + 1) * P], g_words[j][:, t, :, pair], ident[:])
+            xt_of[unit] = xt
+
+        def copy_out(j, pair):
+            if pair == 0:
+                grouped_of[j] = ring.tile(
+                    [P, G * P * PACK], BF16, name="grouped", tag="grouped%d" % (j % GROUPED_BUFS), align_bytes=64
+                )
+            half = 2 * P * PACK
+            nc.scalar.copy(
+                out=grouped_of[j][:, pair * half : (pair + 1) * half].rearrange(
+                    "p (e k t) -> p e k t", e=2, k=P, t=PACK
+                ),
+                in_=xt_of[2 * j + pair][:].bitcast(BF16).rearrange("p (t k e) -> p e k t", t=PACK, k=P, e=2),
+            )
+
+        def front(j, pair):
+            transposes(j, pair)
+            copy_out(j, pair)
+
+        def quantise_g(j):
+            codes = ring.tile([P, G * P], U32, name="g_codes", tag="g_codes%d" % (j % CODES_BUFS), align_bytes=64)
+            scales = ring.tile([P, G * P], U8, name="g_scales", tag="g_scales%d" % (j % CODES_BUFS), align_bytes=64)
+            nc.vector.quantize_mx(out=codes[:].bitcast(E5M2X4), scales=scales[:], in_=grouped_of[j][:])
+            codes_of[j] = (codes, scales)
+
+        def prepare_w(g):
+            w_grouped = ring.tile([P, I * PACK], BF16, name="w_grouped", tag="w_grouped%d" % (g % 2), align_bytes=64)
+            nc.vector.tensor_copy(
+                out=w_grouped[:].rearrange("p (c i t) -> p c t i", i=4, t=PACK),
+                in_=w_raw[g][:].rearrange("p (t c i) -> p c t i", t=PACK, i=4),
+            )
+            nc.vector.quantize_mx(
+                out=w_codes[:, g * I : (g + 1) * I].bitcast(E4M3X4),
+                scales=w_scales[:, g * I : (g + 1) * I],
+                in_=w_grouped[:],
+            )
+
+        def multiply(j, g):
+            unit = G * j + g
+            acc = psum.tile([P, I], F32, name="acc", tag="acc%d" % (unit % ACC_BANKS))
+            codes, scales = codes_of[j]
+            nc.tensor.matmul_mx(
+                out=acc[:],
+                lhsT=codes[:, g * P : (g + 1) * P].bitcast(E5M2X4),
+                lhsT_scale=scales[:, g * P : (g + 1) * P],
+                rhs=w_codes[:, g * I : (g + 1) * I].bitcast(E4M3X4),
+                rhs_scale=w_scales[:, g * I : (g + 1) * I],
+                start=True,
+                stop=True,
+            )
+            acc_of[unit] = acc
+
+        def result(j, g):
+            if j not in stage_of:
+                stage_of[j] = ring.tile([P, G * I], F32, name="stage", tag="stage%d" % (j % STAGE_BUFS))
+            dst = stage_of[j][:, g * I : (g + 1) * I]
+            if scalar_takes_out(j, g):
+                nc.scalar.copy(out=dst, in_=acc_of[G * j + g][:])
+            else:
+                nc.vector.tensor_copy(out=dst, in_=acc_of[G * j + g][:])
+
+        def store(j):
+            nc.sync.dma_start(out=o_rows[:, j, :], in_=stage_of[j][:])
+
+        front(0, 0)
+        front(0, 1)
+        prepare_w(0)
+        quantise_g(0)
+        multiply(0, 0)
+        front(1, 0)
+        front(1, 1)
+        prepare_w(1)
+        prepare_w(2)
+        multiply(0, 1)
+        multiply(0, 2)
+        result(0, 0)
+        result(0, 1)
+        front(2, 0)
+        front(2, 1)
+        prepare_w(3)
+        multiply(0, 3)
+        result(0, 2)
+        result(0, 3)
+        store(0)
+        quantise_g(1)
+        quantise_g(2)
+        for j in range(1, NT):
+            for pair in range(2):
+                if j + AHEAD < NT:
+                    front(j + AHEAD, pair)
+                multiply(j, 2 * pair)
+                multiply(j, 2 * pair + 1)
+            for g in range(G):
+                result(j, g)
+            if j + AHEAD < NT:
+                quantise_g(j + AHEAD)
+            store(j)

@@ -23,8 +23,8 @@ FLOPS = 2 * TOKENS * G * H * I
 BYTES = TOKENS * COLS * 2 + G * H * I * 2 + TOKENS * G * I * 4
 
 LOADS = (
-    ("g", 0, 1), ("w", 0, 1), ("w", 1, 1), ("g", 1, 1), ("w", 2, 1), ("w", 3, 1),
-    ("g", 2, 1), ("g", 3, 1), ("g", 4, 2), ("g", 6, 2), ("g", 8, 4), ("g", 12, 4),
+    ("g", 0, 1), ("w", 0, 1), ("g", 1, 1), ("w", 1, 1), ("w", 2, 1), ("g", 2, 1), ("w", 3, 1),
+    ("g", 3, 1), ("g", 4, 2), ("g", 6, 2), ("g", 8, 4), ("g", 12, 4),
 )
 XT_BANKS = 4
 ACC_BANKS = 4
@@ -35,10 +35,8 @@ AHEAD = 2
 
 
 def scalar_takes_out(j, g):
-    if j == 0:
-        return True
     if j >= NT - 2:
-        return g >= 2
+        return g % 2 == 1
     return g == 3 and j % 2 == 1
 
 
@@ -130,7 +128,7 @@ def tile_groupedlinear_t_kernel(tc, x, W, b, grad_out, out):
 
         def multiply(j, g):
             unit = G * j + g
-            acc = psum.tile([P, I], F32, name="acc", tag="acc%d" % (unit % ACC_BANKS))
+            acc = psum.tile([P, I], F32, name="acc", tag="acc%d" % (len(acc_of) % ACC_BANKS))
             codes, scales = codes_of[j]
             nc.tensor.matmul_mx(
                 out=acc[:],
@@ -143,48 +141,72 @@ def tile_groupedlinear_t_kernel(tc, x, W, b, grad_out, out):
             )
             acc_of[unit] = acc
 
-        def result(j, g):
+        def result(j, g, on_scalar):
             if j not in stage_of:
                 stage_of[j] = ring.tile([P, G * I], F32, name="stage", tag="stage%d" % (j % STAGE_BUFS))
             dst = stage_of[j][:, g * I : (g + 1) * I]
-            if scalar_takes_out(j, g):
+            if on_scalar:
                 nc.scalar.copy(out=dst, in_=acc_of[G * j + g][:])
             else:
                 nc.vector.tensor_copy(out=dst, in_=acc_of[G * j + g][:])
 
-        def store(j):
-            nc.sync.dma_start(out=o_rows[:, j, :], in_=stage_of[j][:])
+        def store(j, first_g, last_g):
+            cols = slice(first_g * I, last_g * I)
+            nc.sync.dma_start(out=o_rows[:, j, cols], in_=stage_of[j][:, cols])
 
         front(0, 0)
         front(0, 1)
         prepare_w(0)
         quantise_g(0)
-        multiply(0, 0)
         front(1, 0)
         front(1, 1)
+        multiply(0, 0)
         prepare_w(1)
-        prepare_w(2)
         multiply(0, 1)
-        multiply(0, 2)
-        result(0, 0)
-        result(0, 1)
-        front(2, 0)
-        front(2, 1)
-        prepare_w(3)
-        multiply(0, 3)
-        result(0, 2)
-        result(0, 3)
-        store(0)
+        result(0, 0, True)
+        result(0, 1, True)
+        transposes(2, 0)
+        transposes(2, 1)
+        copy_out(2, 0)
+        prepare_w(2)
         quantise_g(1)
+        multiply(0, 2)
+        multiply(1, 0)
+        multiply(1, 1)
+        multiply(1, 2)
+        result(0, 2, True)
+        copy_out(2, 1)
+        result(1, 1, True)
+        prepare_w(3)
+        transposes(3, 0)
+        transposes(3, 1)
+        multiply(0, 3)
+        result(1, 0, False)
+        multiply(1, 3)
+        result(1, 2, False)
+        result(0, 3, False)
+        store(0, 0, G)
+        result(1, 3, False)
+        store(1, 0, G)
+        copy_out(3, 0)
+        copy_out(3, 1)
         quantise_g(2)
-        for j in range(1, NT):
-            for pair in range(2):
-                if j + AHEAD < NT:
-                    front(j + AHEAD, pair)
-                multiply(j, 2 * pair)
-                multiply(j, 2 * pair + 1)
+        quantise_g(3)
+        for j in range(2, NT):
+            if j + AHEAD < NT:
+                transposes(j + AHEAD, 0)
+                transposes(j + AHEAD, 1)
+                copy_out(j + AHEAD, 0)
+                copy_out(j + AHEAD, 1)
             for g in range(G):
-                result(j, g)
+                multiply(j, g)
+            for g in range(G):
+                result(j, g, scalar_takes_out(j, g))
+                if j == NT - 1 and g == 1:
+                    store(j, 0, 2)
             if j + AHEAD < NT:
                 quantise_g(j + AHEAD)
-            store(j)
+            if j == NT - 1:
+                store(j, 2, G)
+            else:
+                store(j, 0, G)

@@ -61,16 +61,13 @@ def tile_groupedlinear_t_kernel(tc, x, W, b, grad_out, out):
                     in_=g_rows[:, first : first + count, :],
                 )
                 words = g_in[:].bitcast(F32).rearrange(
-                    "p (n t h q) -> p n t h q", n=count, t=PACK, h=P, q=2
+                    "p (n h t q) -> p n t h q", n=count, h=P, t=PACK, q=2
                 )
                 for n in range(count):
                     g_words[first + n] = words[:, n, :, :, :]
             else:
                 raw = keep.tile([P, PACK * I], BF16, name="w_raw%d" % first)
-                nc.sync.dma_start(
-                    out=raw[:].rearrange("p (t i) -> p t i", t=PACK),
-                    in_=W[first, :, :].rearrange("(t p) i -> p t i", p=P),
-                )
+                nc.sync.dma_start(out=raw[:], in_=W[first, :, :].rearrange("(p t) i -> p (t i)", t=PACK))
                 w_raw[first] = raw
 
         ident = keep.tile([P, P], F32, name="ident")

@@ -30,7 +30,8 @@ XT_BANKS = 4
 ACC_BANKS = 4
 GROUPED_BUFS = 4
 CODES_BUFS = 4
-STAGE_BUFS = 10
+STAGE_BUFS = 6
+STORES = ((0, 2), (2, 2), (4, 2), (6, 2), (8, 2), (10, 2), (12, 1), (13, 1), (14, 1), (15, 1))
 AHEAD = 2
 
 
@@ -138,18 +139,34 @@ def tile_groupedlinear_t_kernel(tc, x, W, b, grad_out, out):
             )
             acc_of[unit] = acc
 
+        store_of = {}
+        for k, (first, count) in enumerate(STORES):
+            for n in range(count):
+                store_of[first + n] = (k, first, count)
+
         def result(j, g, on_scalar):
-            if j not in stage_of:
-                stage_of[j] = ring.tile([P, G * I], F32, name="stage", tag="stage%d" % (j % STAGE_BUFS))
-            dst = stage_of[j][:, g * I : (g + 1) * I]
+            k, first, count = store_of[j]
+            if k not in stage_of:
+                stage_of[k] = ring.tile([P, count * G * I], F32, name="stage", tag="stage%d" % (k % STAGE_BUFS))
+            col = (j - first) * G * I + g * I
+            dst = stage_of[k][:, col : col + I]
             if on_scalar:
                 nc.scalar.copy(out=dst, in_=acc_of[G * j + g][:])
             else:
                 nc.vector.tensor_copy(out=dst, in_=acc_of[G * j + g][:])
 
-        def store(j, first_g, last_g):
-            cols = slice(first_g * I, last_g * I)
-            nc.sync.dma_start(out=o_rows[:, j, cols], in_=stage_of[j][:, cols])
+        def store(j):
+            k, first, count = store_of[j]
+            if j == first + count - 1:
+                nc.sync.dma_start(
+                    out=o_rows[:, first : first + count, :],
+                    in_=stage_of[k][:].rearrange("p (n c) -> p n c", n=count),
+                )
+
+        def store_half(j, half):
+            k, first, count = store_of[j]
+            cols = slice(half * 2 * I, (half + 1) * 2 * I)
+            nc.sync.dma_start(out=o_rows[:, j, cols], in_=stage_of[k][:, cols])
 
         front(0, 0)
         front(0, 1)
@@ -182,9 +199,9 @@ def tile_groupedlinear_t_kernel(tc, x, W, b, grad_out, out):
         multiply(1, 3)
         result(1, 2, False)
         result(0, 3, False)
-        store(0, 0, G)
+        store(0)
         result(1, 3, False)
-        store(1, 0, G)
+        store(1)
         copy_out(3, 0)
         copy_out(3, 1)
         quantise_g(2)
@@ -200,10 +217,10 @@ def tile_groupedlinear_t_kernel(tc, x, W, b, grad_out, out):
             for g in range(G):
                 result(j, g, scalar_takes_out(j, g))
                 if j == NT - 1 and g == 1:
-                    store(j, 0, 2)
+                    store_half(j, 0)
             if j + AHEAD < NT:
                 quantise_g(j + AHEAD)
             if j == NT - 1:
-                store(j, 2, G)
+                store_half(j, 1)
             else:
-                store(j, 0, G)
+                store(j)

@@ -56,7 +56,7 @@ def tile_groupedlinear_t_kernel(tc, x, W, b, grad_out, out):
         w_raw = {}
         for kind, first, count in LOADS:
             if kind == "g":
-                g_in = keep.tile([P, count * COLS], BF16, name="g_in%d" % first)
+                g_in = keep.tile([P, count * COLS], BF16, name="g_in%d" % first, align_bytes=256)
                 nc.sync.dma_start(
                     out=g_in[:].rearrange("p (n c) -> p n c", n=count),
                     in_=g_rows[:, first : first + count, :],
@@ -67,7 +67,7 @@ def tile_groupedlinear_t_kernel(tc, x, W, b, grad_out, out):
                 for n in range(count):
                     g_words[first + n] = words[:, n, :, :, :]
             else:
-                raw = keep.tile([P, PACK * I], BF16, name="w_raw%d" % first)
+                raw = keep.tile([P, PACK * I], BF16, name="w_raw%d" % first, align_bytes=256)
                 nc.sync.dma_start(out=raw[:], in_=W[first, :, :].rearrange("(p t) i -> p (t i)", t=PACK))
                 w_raw[first] = raw
 
@@ -147,7 +147,9 @@ def tile_groupedlinear_t_kernel(tc, x, W, b, grad_out, out):
         def result(j, g, on_scalar):
             k, first, count = store_of[j]
             if k not in stage_of:
-                stage_of[k] = ring.tile([P, count * G * I], F32, name="stage", tag="stage%d" % (k % STAGE_BUFS))
+                stage_of[k] = ring.tile(
+                    [P, count * G * I], F32, name="stage", tag="stage%d" % (k % STAGE_BUFS), align_bytes=256
+                )
             col = (j - first) * G * I + g * I
             dst = stage_of[k][:, col : col + I]
             if on_scalar:

@@ -24,14 +24,14 @@ BYTES = TOKENS * COLS * 2 + G * H * I * 2 + TOKENS * G * I * 4
 
 LOADS = (
     ("g", 0, 1), ("w", 0, 1), ("g", 1, 1), ("w", 1, 1), ("w", 2, 1), ("g", 2, 1), ("w", 3, 1),
-    ("g", 3, 1), ("g", 4, 2), ("g", 6, 2), ("g", 8, 4), ("g", 12, 4),
+    ("g", 3, 1), ("g", 4, 2), ("g", 6, 2), ("g", 8, 8),
 )
 XT_BANKS = 4
 ACC_BANKS = 4
 GROUPED_BUFS = 4
 CODES_BUFS = 4
-STAGE_BUFS = 6
-STORES = ((0, 2), (2, 2), (4, 2), (6, 2), (8, 2), (10, 2), (12, 1), (13, 1), (14, 1), (15, 1))
+STAGE_BUFS = 5
+STORES = ((0, 3), (3, 3), (6, 2), (8, 2), (10, 2), (12, 1), (13, 1), (14, 2))
 AHEAD = 2
 
 
@@ -165,11 +165,6 @@ def tile_groupedlinear_t_kernel(tc, x, W, b, grad_out, out):
                     in_=stage_of[k][:].rearrange("p (n c) -> p n c", n=count),
                 )
 
-        def store_half(j, half):
-            k, first, count = store_of[j]
-            cols = slice(half * 2 * I, (half + 1) * 2 * I)
-            nc.sync.dma_start(out=o_rows[:, j, cols], in_=stage_of[k][:, cols])
-
         front(0, 0)
         front(0, 1)
         prepare_w(0)
@@ -218,11 +213,6 @@ def tile_groupedlinear_t_kernel(tc, x, W, b, grad_out, out):
                 multiply(j, g)
             for g in range(G):
                 result(j, g, scalar_takes_out(j, g))
-                if j == NT - 1 and g == 1:
-                    store_half(j, 0)
             if j + AHEAD < NT:
                 quantise_g(j + AHEAD)
-            if j == NT - 1:
-                store_half(j, 1)
-            else:
-                store(j)
+            store(j)

@@ -23,15 +23,15 @@ FLOPS = 2 * TOKENS * G * H * I
 BYTES = TOKENS * COLS * 2 + G * H * I * 2 + TOKENS * G * I * 4
 
 LOADS = (
-    ("g", 0, 1), ("w", 0, 1), ("g", 1, 1), ("w", 1, 1), ("w", 2, 1), ("g", 2, 1), ("w", 3, 1),
-    ("g", 3, 1), ("g", 4, 2), ("g", 6, 2), ("g", 8, 8),
+    ("g", 0, 1), ("w", 0, 1), ("g", 1, 1), ("w", 1, 2), ("g", 2, 2), ("w", 3, 1),
+    ("g", 4, 4), ("g", 8, 8),
 )
 XT_BANKS = 4
 ACC_BANKS = 4
 GROUPED_BUFS = 4
 CODES_BUFS = 4
 STAGE_BUFS = 5
-STORES = ((0, 3), (3, 3), (6, 2), (8, 2), (10, 2), (12, 1), (13, 1), (14, 2))
+STORES = ((0, 3), (3, 3), (6, 2), (8, 2), (10, 2), (12, 2), (14, 2))
 AHEAD = 2
 
 
@@ -67,9 +67,13 @@ def tile_groupedlinear_t_kernel(tc, x, W, b, grad_out, out):
                 for n in range(count):
                     g_words[first + n] = words[:, n, :, :, :]
             else:
-                raw = keep.tile([P, PACK * I], BF16, name="w_raw%d" % first, align_bytes=256)
-                nc.sync.dma_start(out=raw[:], in_=W[first, :, :].rearrange("(p t) i -> p (t i)", t=PACK))
-                w_raw[first] = raw
+                raw = keep.tile([P, count * PACK * I], BF16, name="w_raw%d" % first, align_bytes=256)
+                nc.sync.dma_start(
+                    out=raw[:].rearrange("p (n c) -> p n c", n=count),
+                    in_=W[first : first + count, :, :].rearrange("n (p t) i -> p n (t i)", t=PACK),
+                )
+                for n in range(count):
+                    w_raw[first + n] = raw[:, n * PACK * I : (n + 1) * PACK * I]
 
         ident = keep.tile([P, P], F32, name="ident")
         make_identity(nc, ident[:])
@@ -116,7 +120,7 @@ def tile_groupedlinear_t_kernel(tc, x, W, b, grad_out, out):
             w_grouped = ring.tile([P, I * PACK], BF16, name="w_grouped", tag="w_grouped%d" % (g % 2), align_bytes=64)
             nc.vector.tensor_copy(
                 out=w_grouped[:].rearrange("p (c i t) -> p c t i", i=4, t=PACK),
-                in_=w_raw[g][:].rearrange("p (t c i) -> p c t i", t=PACK, i=4),
+                in_=w_raw[g].rearrange("p (t c i) -> p c t i", t=PACK, i=4),
             )
             nc.vector.quantize_mx(
                 out=w_codes[:, g * I : (g + 1) * I].bitcast(E4M3X4),

from contextlib import ExitStack

import concourse.mybir as mybir
from concourse.masks import make_identity

F32 = mybir.dt.float32
BF16 = mybir.dt.bfloat16
U32 = mybir.dt.uint32
U8 = mybir.dt.uint8
E4M3X4 = mybir.dt.float8_e4m3fn_x4
E5M2X4 = mybir.dt.float8_e5m2_x4

P = 128
PACK = 4
G = 4
H = 512
I = 512
TOKENS = 2048
NT = TOKENS // P
COLS = G * H

FLOPS = 2 * TOKENS * G * H * I
BYTES = TOKENS * COLS * 2 + G * H * I * 2 + TOKENS * G * I * 4

LOADS = (
    ("g", 0, 1), ("w", 0, 1), ("g", 1, 1), ("w", 1, 2), ("g", 2, 2), ("w", 3, 1),
    ("g", 4, 4), ("g", 8, 8),
)
XT_BANKS = 4
ACC_BANKS = 4
GROUPED_BUFS = 4
CODES_BUFS = 4
STAGE_BUFS = 5
STORES = ((0, 3), (3, 3), (6, 2), (8, 2), (10, 2), (12, 2), (14, 2))
AHEAD = 2


def scalar_takes_out(j, g):
    if j >= NT - 2:
        return g % 2 == 1
    return g == 3 and j % 2 == 1


def tile_groupedlinear_t_kernel(tc, x, W, b, grad_out, out):
    nc = tc.nc
    g_rows = grad_out.flatten_outer_dims().rearrange("(p j) c -> p j c", j=NT)
    o_rows = out.flatten_outer_dims().rearrange("(p j) c -> p j c", j=NT)

    with ExitStack() as ctx:
        keep = ctx.enter_context(tc.tile_pool(name="keep", bufs=1))
        ring = ctx.enter_context(tc.tile_pool(name="ring", bufs=1))
        psum = ctx.enter_context(tc.psum_pool(name="psum", bufs=1))
        ctx.enter_context(tc.manual_schedule())

        g_words = {}
        w_raw = {}
        for kind, first, count in LOADS:
            if kind == "g":
                g_in = keep.tile([P, count * COLS], BF16, name="g_in%d" % first, align_bytes=256)
                nc.sync.dma_start(
                    out=g_in[:].rearrange("p (n c) -> p n c", n=count),
                    in_=g_rows[:, first : first + count, :],
                )
                words = g_in[:].bitcast(F32).rearrange(
                    "p (n h t q) -> p n t h q", n=count, h=P, t=PACK, q=2
                )
                for n in range(count):
                    g_words[first + n] = words[:, n, :, :, :]
            else:
                raw = keep.tile([P, count * PACK * I], BF16, name="w_raw%d" % first, align_bytes=256)
                nc.sync.dma_start(
                    out=raw[:].rearrange("p (n c) -> p n c", n=count),
                    in_=W[first : first + count, :, :].rearrange("n (p t) i -> p n (t i)", t=PACK),
                )
                for n in range(count):
                    w_raw[first + n] = raw[:, n * PACK * I : (n + 1) * PACK * I]

        ident = keep.tile([P, P], F32, name="ident")
        make_identity(nc, ident[:])
        w_codes = keep.tile([P, G * I], U32, name="w_codes", align_bytes=64)
        w_scales = keep.tile([P, G * I], U8, name="w_scales", align_bytes=64)

        xt_of = {}
        grouped_of = {}
        codes_of = {}
        acc_of = {}
        stage_of = {}

        def transposes(j, pair):
            unit = 2 * j + pair
            xt = psum.tile([P, PACK * P], F32, name="xt", tag="xt%d" % (unit % XT_BANKS))
            for t in range(PACK):
                nc.tensor.transpose(xt[:, t * P : (t + 1) * P], g_words[j][:, t, :, pair], ident[:])
            xt_of[unit] = xt

        def copy_out(j, pair):
            if pair == 0:
                grouped_of[j] = ring.tile(
                    [P, G * P * PACK], BF16, name="grouped", tag="grouped%d" % (j % GROUPED_BUFS), align_bytes=64
                )
            half = 2 * P * PACK
            nc.scalar.copy(
                out=grouped_of[j][:, pair * half : (pair + 1) * half].rearrange(
                    "p (e k t) -> p e k t", e=2, k=P, t=PACK
                ),
                in_=xt_of[2 * j + pair][:].bitcast(BF16).rearrange("p (t k e) -> p e k t", t=PACK, k=P, e=2),
            )

        def front(j, pair):
            transposes(j, pair)
            copy_out(j, pair)

        def quantise_g(j):
            codes = ring.tile([P, G * P], U32, name="g_codes", tag="g_codes%d" % (j % CODES_BUFS), align_bytes=64)
            scales = ring.tile([P, G * P], U8, name="g_scales", tag="g_scales%d" % (j % CODES_BUFS), align_bytes=64)
            nc.vector.quantize_mx(out=codes[:].bitcast(E5M2X4), scales=scales[:], in_=grouped_of[j][:])
            codes_of[j] = (codes, scales)

        def prepare_w(g):
            w_grouped = ring.tile([P, I * PACK], BF16, name="w_grouped", tag="w_grouped%d" % (g % 2), align_bytes=64)
            nc.vector.tensor_copy(
                out=w_grouped[:].rearrange("p (c i t) -> p c t i", i=4, t=PACK),
                in_=w_raw[g].rearrange("p (t c i) -> p c t i", t=PACK, i=4),
            )
            nc.vector.quantize_mx(
                out=w_codes[:, g * I : (g + 1) * I].bitcast(E4M3X4),
                scales=w_scales[:, g * I : (g + 1) * I],
                in_=w_grouped[:],
            )

        def multiply(j, g):
            unit = G * j + g
            acc = psum.tile([P, I], F32, name="acc", tag="acc%d" % (len(acc_of) % ACC_BANKS))
            codes, scales = codes_of[j]
            nc.tensor.matmul_mx(
                out=acc[:],
                lhsT=codes[:, g * P : (g + 1) * P].bitcast(E5M2X4),
                lhsT_scale=scales[:, g * P : (g + 1) * P],
                rhs=w_codes[:, g * I : (g + 1) * I].bitcast(E4M3X4),
                rhs_scale=w_scales[:, g * I : (g + 1) * I],
                start=True,
                stop=True,
            )
            acc_of[unit] = acc

        store_of = {}
        for k, (first, count) in enumerate(STORES):
            for n in range(count):
                store_of[first + n] = (k, first, count)

        def result(j, g, on_scalar):
            k, first, count = store_of[j]
            if k not in stage_of:
                stage_of[k] = ring.tile(
                    [P, count * G * I], F32, name="stage", tag="stage%d" % (k % STAGE_BUFS), align_bytes=256
                )
            col = (j - first) * G * I + g * I
            dst = stage_of[k][:, col : col + I]
            if on_scalar:
                nc.scalar.copy(out=dst, in_=acc_of[G * j + g][:])
            else:
                nc.vector.tensor_copy(out=dst, in_=acc_of[G * j + g][:])

        def store(j):
            k, first, count = store_of[j]
            if j == first + count - 1:
                nc.sync.dma_start(
                    out=o_rows[:, first : first + count, :],
                    in_=stage_of[k][:].rearrange("p (n c) -> p n c", n=count),
                )

        front(0, 0)
        front(0, 1)
        prepare_w(0)
        quantise_g(0)
        front(1, 0)
        front(1, 1)
        multiply(0, 0)
        prepare_w(1)
        multiply(0, 1)
        result(0, 0, True)
        result(0, 1, True)
        transposes(2, 0)
        transposes(2, 1)
        copy_out(2, 0)
        prepare_w(2)
        quantise_g(1)
        multiply(0, 2)
        multiply(1, 0)
        multiply(1, 1)
        multiply(1, 2)
        result(0, 2, True)
        copy_out(2, 1)
        result(1, 1, True)
        prepare_w(3)
        transposes(3, 0)
        transposes(3, 1)
        multiply(0, 3)
        result(1, 0, False)
        multiply(1, 3)
        result(1, 2, False)
        result(0, 3, False)
        store(0)
        result(1, 3, False)
        store(1)
        copy_out(3, 0)
        copy_out(3, 1)
        quantise_g(2)
        quantise_g(3)
        for j in range(2, NT):
            if j + AHEAD < NT:
                transposes(j + AHEAD, 0)
                transposes(j + AHEAD, 1)
                copy_out(j + AHEAD, 0)
                copy_out(j + AHEAD, 1)
            for g in range(G):
                multiply(j, g)
            for g in range(G):
                result(j, g, scalar_takes_out(j, g))
            if j + AHEAD < NT:
                quantise_g(j + AHEAD)
            store(j)
